import numpy as np
import ml_dtypes


def mxq(x, axis, fmt="e4m3"):
    dtype, down = {"e4m3": (ml_dtypes.float8_e4m3fn, 7), "e5m2": (ml_dtypes.float8_e5m2, 14)}[fmt]
    v = np.moveaxis(np.asarray(x, np.float32).astype(ml_dtypes.bfloat16).astype(np.float64), axis, -1)
    blocks = v.reshape(v.shape[:-1] + (-1, 32))
    amax = np.abs(blocks).max(-1, keepdims=True)
    byte = np.maximum(np.where(amax > 0, np.frexp(amax)[1] - 1 + 127, 0) - down, 1)
    scale = np.exp2(byte - 127.0)
    codes = (blocks / scale).astype(np.float32).astype(dtype).astype(np.float64)
    return np.moveaxis((codes * scale).reshape(v.shape), -1, axis)


WIDE = False


def mx_kscale(k):
    if not WIDE:
        return np.ones(k)
    levels = np.array([10, -10, 5, -5, 0])
    a = np.random.permutation(np.resize(levels, k // 512 * 4)).reshape(k // 512, 4)
    idx = np.arange(k)
    return np.exp2(a[idx // 512, idx % 128 // 32])


BF16 = ml_dtypes.bfloat16


def bf(x):
    return np.asarray(x, np.float32).astype(BF16)


def f64(x):
    return np.asarray(x).astype(np.float64)


E2M1 = np.array([0.0, 0.5, 1.0, 1.5, 2.0, 3.0, 4.0, 6.0, -0.0, -0.5, -1.0, -1.5, -2.0, -3.0, -4.0, -6.0])


def pack_weight(w, fmt):
    k, n = w.shape
    w = f64(bf(w)).reshape(k // 32, 32, n)
    amax = np.abs(w).max(1)
    if fmt == "e4m3":
        byte = np.frexp(amax)[1] - 1 + 127 - 7
    else:
        mant, ex = np.frexp(amax / 6.0)
        byte = np.where(mant > 0.5, ex, ex - 1) + 127
    byte = np.clip(np.where(amax > 0, byte, 1), 1, 254)
    scaled = (w * np.exp2(127.0 - byte)[:, None, :]).reshape(k, n).astype(np.float32)
    by_word = np.ascontiguousarray(scaled.reshape(k // 512, 128, 4, n).transpose(0, 1, 3, 2))
    if fmt == "e4m3":
        words = by_word.astype(ml_dtypes.float8_e4m3fn).view(np.uint8)
    else:
        c = by_word.astype(ml_dtypes.float4_e2m1fn).view(np.uint8) & 0xF
        words = c[..., 0::2] | (c[..., 1::2] << 4)
    return np.ascontiguousarray(words), np.ascontiguousarray(byte.astype(np.uint8).reshape(k // 512, 16, n))


def unpack_weight(words, scales, fmt):
    g, p, n, _ = words.shape
    if fmt == "e4m3":
        vals = np.ascontiguousarray(words).view(ml_dtypes.float8_e4m3fn).astype(np.float64)
    else:
        nib = np.empty((g, p, n, 4), np.uint8)
        nib[..., 0::2] = words & 0xF
        nib[..., 1::2] = words >> 4
        vals = E2M1[nib]
    vals = vals * np.repeat(np.exp2(scales.astype(np.float64) - 127.0), 8, axis=1)[..., None]
    return vals.transpose(0, 1, 3, 2).reshape(g * 512, n)

def pack4(w):
    words, scales = pack_weight(w, "e2m1")
    return words.reshape(words.shape[0], 128, -1), scales


def unpack4(words, scales):
    return unpack_weight(words.reshape(words.shape[0], 128, -1, 2), scales, "e2m1")


B, C, S, OUT = 256, 4, 64, 128
IN = C * S * S
HS = S // 2
SUB, BLK = 4, 32


def haar_dwt2_features(x):
    x4 = x.reshape(x.shape[0], C, S, S)
    a = x4[:, :, 0::2, 0::2]
    bq = x4[:, :, 0::2, 1::2]
    c = x4[:, :, 1::2, 0::2]
    d = x4[:, :, 1::2, 1::2]
    LL = (a + bq + c + d) * 0.5
    LH = (a + bq - c - d) * 0.5
    HL = (a - bq + c - d) * 0.5
    HH = (a - bq - c + d) * 0.5
    t = np.stack([LL, LH, HL, HH], axis=2)
    return t.reshape(x.shape[0], -1)


def setup_inputs():
    g = mx_kscale(IN).reshape(-1, SUB, BLK)[:, 0, :].reshape(C, HS, HS)
    gx = np.repeat(np.repeat(g, 2, axis=1), 2, axis=2).reshape(IN)
    gt = np.repeat(g[:, None], SUB, axis=1).reshape(IN)
    x = bf(np.random.standard_normal((B, IN)) * gx)
    w = np.random.standard_normal((OUT, IN)) * (1.0 / np.sqrt(IN)) / gt
    words, scales = pack4(np.ascontiguousarray(w.T))
    b = bf(np.random.standard_normal(OUT) * 0.5)
    return {"x": x, "W_words": words, "W_scales": scales, "b": b}


def reference(x, W_words, W_scales, b):
    t = haar_dwt2_features(f64(x))
    return (mxq(t, 1, "e4m3") @ unpack4(W_words, W_scales)) + f64(b)

@@ -1,0 +1,209 @@
+from contextlib import ExitStack
+
+import concourse.mybir as mybir
+from concourse.masks import make_identity
+
+F32 = mybir.dt.float32
+BF16 = mybir.dt.bfloat16
+I32 = mybir.dt.int32
+U32 = mybir.dt.uint32
+U8 = mybir.dt.uint8
+FP8X4 = mybir.dt.float8_e4m3fn_x4
+FP4X4 = mybir.dt.float4_e2m1fn_x4
+ADD = mybir.AluOpType.add
+SUBTRACT = mybir.AluOpType.subtract
+COPY = mybir.ActivationFunctionType.Copy
+
+P = 128
+PACK = 4
+K_PASS = P * PACK
+
+BATCH, CHANNELS, SIDE, OUT = 256, 4, 64, 128
+HALF_SIDE = SIDE // 2
+PIXELS = SIDE * SIDE
+BAND = HALF_SIDE * HALF_SIDE
+SUBBANDS = 4
+PASSES = CHANNELS * SUBBANDS * BAND // K_PASS
+BAND_PASSES = BAND // K_PASS
+PASS_ROWS = HALF_SIDE // BAND_PASSES
+PASS_PIXELS = PIXELS // BAND_PASSES
+ROW_TILES = BATCH // P
+WORDS_PER_ROW = HALF_SIDE // PACK
+EVEN, ODD = 0, 1
+
+SIGNS = 2
+TILE_STAGES = CHANNELS * BAND_PASSES * SIGNS
+STAGES = ROW_TILES * TILE_STAGES
+STAGE_PASSES = 2
+RUN_STAGES = 8
+KEEP_ALIVE_EVERY = 21
+EARLY_PIECES = 5
+HEAD_CHUNKS = 4
+
+NEGATE_LAG = 1
+TRANSPOSE_LAG = 2
+QUANTISE_LAG = 4
+FINISH_LAG = 6
+
+FLOPS = 2 * BATCH * CHANNELS * PIXELS * OUT
+
+
+def tile_waveletlinearlayer_kernel(tc, x, W_words, W_scales, b, out):
+    nc = tc.nc
+    with ExitStack() as ctx:
+        const = ctx.enter_context(tc.tile_pool(name="const", bufs=1))
+        step1 = ctx.enter_context(tc.tile_pool(name="step1", bufs=5))
+        packed = ctx.enter_context(tc.tile_pool(name="packed", bufs=14))
+        results = ctx.enter_context(tc.tile_pool(name="results", bufs=2))
+        banks = ctx.enter_context(tc.psum_pool(name="banks", bufs=6))
+        sums = ctx.enter_context(tc.psum_pool(name="sums", bufs=1))
+        spare = ctx.enter_context(tc.psum_pool(name="spare", bufs=1))
+        ctx.enter_context(tc.manual_schedule())
+
+        identity = const.tile([P, P], F32)
+        make_identity(nc, identity[:])
+
+        pixel_tiles = {}
+
+        def load_pixels(piece):
+            row_tile, columns = divmod(piece, CHANNELS * BAND_PASSES)
+            chunks = HEAD_CHUNKS if piece == 0 else 1
+            width = PASS_PIXELS // chunks
+            pixel_tiles[piece] = []
+            for chunk in range(chunks):
+                pixels = const.tile([P, width], BF16, name="pixels_%d_%d" % (piece, chunk))
+                first = columns * PASS_PIXELS + chunk * width
+                nc.sync.dma_start(out=pixels[:], in_=x[row_tile * P : (row_tile + 1) * P, first : first + width])
+                pixel_tiles[piece].append(pixels)
+
+        w_scales = const.tile([P, PASSES, OUT], U8, align_bytes=64)
+        nc.vector.memset(w_scales[:].bitcast(I32), 0)
+        w_codes = const.tile([P, PASSES, 2 * OUT], U8, align_bytes=64)
+        bias = const.tile([P, OUT], BF16)
+
+        for piece in range(EARLY_PIECES):
+            load_pixels(piece)
+        for quadrant in range(4):
+            nc.sync.dma_start(
+                out=w_scales[32 * quadrant : 32 * quadrant + 4].bitcast(I32),
+                in_=W_scales[:, 4 * quadrant : 4 * quadrant + 4, :].bitcast(I32).rearrange("g r w -> r g w"),
+            )
+        nc.sync.dma_start(out=w_codes[:].bitcast(I32), in_=W_words.bitcast(I32).rearrange("g p w -> p g w"))
+        for piece in range(EARLY_PIECES, STAGES // SIGNS):
+            load_pixels(piece)
+        nc.sync.dma_start(out=bias[:], in_=b.partition_broadcast(P))
+
+        def pair_columns(stage):
+            piece, sign = divmod(stage, SIGNS)
+            paired = step1.tile([P, 2, PACK, P], F32)
+            planes = paired[:].rearrange("n r t (i c) -> n r i c t", c=WORDS_PER_ROW)
+            rows = PASS_ROWS // len(pixel_tiles[piece])
+            for chunk, chunk_tile in enumerate(pixel_tiles[piece]):
+                pixels = chunk_tile[:].rearrange(
+                    "n (i r c t e) -> n e r i c t", i=rows, r=2, c=WORDS_PER_ROW, t=PACK, e=2
+                )
+                nc.vector.tensor_tensor(
+                    out=planes[:, :, chunk * rows : (chunk + 1) * rows],
+                    in0=pixels[:, 0],
+                    in1=pixels[:, 1],
+                    op=(ADD if sign == 0 else SUBTRACT),
+                )
+            return paired
+
+        def negate(odd):
+            minus_odd = step1.tile([P, PACK, P], F32)
+            nc.scalar.activation(out=minus_odd[:], in_=odd, func=COPY, scale=-1.0)
+            return minus_odd
+
+        unread = spare.tile([P, P], F32)
+        transposes_issued = [0]
+
+        def keep_clock_up():
+            transposes_issued[0] += 1
+            if transposes_issued[0] % KEEP_ALIVE_EVERY == 0:
+                nc.tensor.matmul(out=unread[:], lhsT=identity[:], rhs=identity[:], start=True, stop=True)
+
+        def transpose_and_add(first, second, target):
+            bank = banks.tile([P, PACK, P], F32)
+            for t in range(PACK):
+                for addend in (first, second):
+                    nc.tensor.matmul(
+                        out=bank[:, t, :], lhsT=addend[:, t, :], rhs=identity[:], is_transpose=True,
+                        start=(addend is first), stop=(addend is second),
+                    )
+                    keep_clock_up()
+            nc.scalar.activation(out=target, in_=bank[:].rearrange("p t n -> p n t"), func=COPY, scale=0.5)
+
+        def quantise(grouped):
+            t_codes = packed.tile([P, STAGE_PASSES, P], U32, align_bytes=64)
+            t_scales = packed.tile([P, STAGE_PASSES, P], U8, align_bytes=64)
+            nc.vector.quantize_mx(
+                out=t_codes[:].rearrange("p s n -> p (s n)").bitcast(FP8X4),
+                scales=t_scales[:].rearrange("p s n -> p (s n)"),
+                in_=grouped[:].rearrange("p s n t -> p (s n t)"),
+            )
+            return t_codes, t_scales
+
+        sum_tiles = {}
+
+        def multiply(stage, t_codes, t_scales):
+            row_tile, tile_stage = divmod(stage, TILE_STAGES)
+            channel, rest = divmod(tile_stage, BAND_PASSES * SIGNS)
+            half, sign = divmod(rest, SIGNS)
+            if tile_stage == 0:
+                sum_tiles[row_tile] = sums.tile([P, OUT], F32, name="batch_sum")
+            for difference in range(STAGE_PASSES):
+                subband = 2 * sign + difference
+                g = (channel * SUBBANDS + subband) * BAND_PASSES + half
+                nc.tensor.matmul_mx(
+                    out=sum_tiles[row_tile][:],
+                    lhsT=t_codes[:, difference, :].bitcast(FP8X4),
+                    lhsT_scale=t_scales[:, difference, :],
+                    rhs=w_codes[:, g, :].bitcast(FP4X4),
+                    rhs_scale=w_scales[:, g, :],
+                    start=(tile_stage == 0 and difference == 0),
+                    stop=(tile_stage == TILE_STAGES - 1 and difference == STAGE_PASSES - 1),
+                )
+
+        def finish(row_tile):
+            result = results.tile([P, OUT], F32)
+            nc.vector.tensor_tensor(out=result[:], in0=sum_tiles[row_tile][:], in1=bias[:], op=ADD)
+            nc.sync.dma_start(out=out[row_tile * P : (row_tile + 1) * P, :], in_=result[:])
+
+        paired_tiles, minus_odds, grouped_tiles, code_tiles = {}, {}, {}, {}
+        waiting = []
+
+        for turn in range(STAGES + FINISH_LAG + 1):
+            stage = turn - QUANTISE_LAG
+            if 0 <= stage < STAGES:
+                code_tiles[stage] = quantise(grouped_tiles[stage])
+                waiting.append(stage)
+            if turn >= STAGES + TRANSPOSE_LAG:
+                run = len(waiting)
+            elif len(waiting) > RUN_STAGES:
+                run = RUN_STAGES
+            else:
+                run = 0
+            for ready in waiting[:run]:
+                multiply(ready, code_tiles[ready][0], code_tiles[ready][1])
+            waiting = waiting[run:]
+
+            stage = turn - FINISH_LAG
+            if stage >= 0 and (stage + 1) % TILE_STAGES == 0:
+                finish(stage // TILE_STAGES)
+
+            stage = turn
+            if stage < STAGES:
+                paired_tiles[stage] = pair_columns(stage)
+
+            stage = turn - NEGATE_LAG
+            if 0 <= stage < STAGES:
+                minus_odds[stage] = negate(paired_tiles[stage][:, ODD])
+
+            stage = turn - TRANSPOSE_LAG
+            if 0 <= stage < STAGES:
+                even, odd = paired_tiles[stage][:, EVEN], paired_tiles[stage][:, ODD]
+                grouped = packed.tile([P, STAGE_PASSES, P, PACK], BF16, align_bytes=64)
+                grouped_tiles[stage] = grouped
+                transpose_and_add(even, odd, grouped[:, 0])
+                transpose_and_add(even, minus_odds[stage][:], grouped[:, 1])

@@ -36,7 +36,8 @@ TILE_STAGES = CHANNELS * BAND_PASSES * SIGNS
 STAGES = ROW_TILES * TILE_STAGES
 STAGE_PASSES = 2
 RUN_STAGES = 8
-KEEP_ALIVE_EVERY = 21
+KEEP_ALIVE_COLUMNS = 64
+WARM_UP_MATMULS = 7
 EARLY_PIECES = 5
 HEAD_CHUNKS = 4
 
@@ -116,12 +117,11 @@ def tile_waveletlinearlayer_kernel(tc, x, W_words, W_scales, b, out):
             return minus_odd
 
         unread = spare.tile([P, P], F32)
-        transposes_issued = [0]
 
-        def keep_clock_up():
-            transposes_issued[0] += 1
-            if transposes_issued[0] % KEEP_ALIVE_EVERY == 0:
-                nc.tensor.matmul(out=unread[:], lhsT=identity[:], rhs=identity[:], start=True, stop=True)
+        def keep_clock_up(columns):
+            nc.tensor.matmul(
+                out=unread[:, :columns], lhsT=identity[:], rhs=identity[:, :columns], start=True, stop=True
+            )
 
         def transpose_and_add(first, second, target):
             bank = banks.tile([P, PACK, P], F32)
@@ -131,7 +131,6 @@ def tile_waveletlinearlayer_kernel(tc, x, W_words, W_scales, b, out):
                         out=bank[:, t, :], lhsT=addend[:, t, :], rhs=identity[:], is_transpose=True,
                         start=(addend is first), stop=(addend is second),
                     )
-                    keep_clock_up()
             nc.scalar.activation(out=target, in_=bank[:].rearrange("p t n -> p n t"), func=COPY, scale=0.5)
 
         def quantise(grouped):
@@ -173,6 +172,8 @@ def tile_waveletlinearlayer_kernel(tc, x, W_words, W_scales, b, out):
         paired_tiles, minus_odds, grouped_tiles, code_tiles = {}, {}, {}, {}
         waiting = []
 
+        for warm_up in range(WARM_UP_MATMULS):
+            keep_clock_up(P)
         for turn in range(STAGES + FINISH_LAG + 1):
             stage = turn - QUANTISE_LAG
             if 0 <= stage < STAGES:
@@ -207,3 +208,4 @@ def tile_waveletlinearlayer_kernel(tc, x, W_words, W_scales, b, out):
                 grouped_tiles[stage] = grouped
                 transpose_and_add(even, odd, grouped[:, 0])
                 transpose_and_add(even, minus_odds[stage][:], grouped[:, 1])
+                keep_clock_up(KEEP_ALIVE_COLUMNS)

@@ -11,6 +11,7 @@ U8 = mybir.dt.uint8
 FP8X4 = mybir.dt.float8_e4m3fn_x4
 FP4X4 = mybir.dt.float4_e2m1fn_x4
 ADD = mybir.AluOpType.add
+MULT = mybir.AluOpType.mult
 SUBTRACT = mybir.AluOpType.subtract
 COPY = mybir.ActivationFunctionType.Copy
 
@@ -131,7 +132,7 @@ def tile_waveletlinearlayer_kernel(tc, x, W_words, W_scales, b, out):
                         out=bank[:, t, :], lhsT=addend[:, t, :], rhs=identity[:], is_transpose=True,
                         start=(addend is first), stop=(addend is second),
                     )
-            nc.scalar.activation(out=target, in_=bank[:].rearrange("p t n -> p n t"), func=COPY, scale=0.5)
+            nc.scalar.copy(out=target, in_=bank[:].rearrange("p t n -> p n t"))
 
         def quantise(grouped):
             t_codes = packed.tile([P, STAGE_PASSES, P], U32, align_bytes=64)
@@ -166,7 +167,9 @@ def tile_waveletlinearlayer_kernel(tc, x, W_words, W_scales, b, out):
 
         def finish(row_tile):
             result = results.tile([P, OUT], F32)
-            nc.vector.tensor_tensor(out=result[:], in0=sum_tiles[row_tile][:], in1=bias[:], op=ADD)
+            nc.vector.scalar_tensor_tensor(
+                out=result[:], in0=sum_tiles[row_tile][:], scalar=0.5, in1=bias[:], op0=MULT, op1=ADD
+            )
             nc.sync.dma_start(out=out[row_tile * P : (row_tile + 1) * P, :], in_=result[:])
 
         paired_tiles, minus_odds, grouped_tiles, code_tiles = {}, {}, {}, {}

@@ -37,6 +37,7 @@ TILE_STAGES = CHANNELS * BAND_PASSES * SIGNS
 STAGES = ROW_TILES * TILE_STAGES
 STAGE_PASSES = 2
 RUN_STAGES = 8
+VECTOR_NEGATES_EVERY = 8
 KEEP_ALIVE_COLUMNS = 64
 WARM_UP_MATMULS = 7
 EARLY_PIECES = 5
@@ -55,6 +56,7 @@ def tile_waveletlinearlayer_kernel(tc, x, W_words, W_scales, b, out):
     with ExitStack() as ctx:
         const = ctx.enter_context(tc.tile_pool(name="const", bufs=1))
         step1 = ctx.enter_context(tc.tile_pool(name="step1", bufs=5))
+        step12 = ctx.enter_context(tc.tile_pool(name="step12", bufs=1))
         packed = ctx.enter_context(tc.tile_pool(name="packed", bufs=14))
         results = ctx.enter_context(tc.tile_pool(name="results", bufs=2))
         banks = ctx.enter_context(tc.psum_pool(name="banks", bufs=6))
@@ -112,9 +114,51 @@ def tile_waveletlinearlayer_kernel(tc, x, W_words, W_scales, b, out):
                 )
             return paired
 
-        def negate(odd):
+        def on_vector(stage):
+            return stage == STAGES - 1
+
+        def pair_columns_in_rows(stage):
+            piece, sign = divmod(stage, SIGNS)
+            rows = step12.tile([P, PASS_ROWS, 2, HALF_SIDE], F32)
+            pixels = pixel_tiles[piece][0][:].rearrange("n (k e) -> n e k", e=2)
+            nc.vector.tensor_tensor(
+                out=rows[:].rearrange("n i r j -> n (i r j)"), in0=pixels[:, 0], in1=pixels[:, 1],
+                op=(ADD if sign == 0 else SUBTRACT),
+            )
+            return rows
+
+        def add_rows(rows):
+            features = step12.tile([P, STAGE_PASSES, K_PASS], BF16, align_bytes=64)
+            for difference in range(STAGE_PASSES):
+                nc.vector.tensor_tensor(
+                    out=features[:, difference].rearrange("n (i j) -> n i j", j=HALF_SIDE),
+                    in0=rows[:, :, EVEN], in1=rows[:, :, ODD], op=(SUBTRACT if difference else ADD),
+                )
+            return features
+
+        def transpose_words(features, grouped):
+            words = features[:].rearrange("n d k -> n (d k)").bitcast(F32)
+            bank = banks.tile([P, PACK, P], F32)
+            for difference in range(STAGE_PASSES):
+                for u in range(2):
+                    first = difference * K_PASS // 2 + u
+                    nc.tensor.matmul(
+                        out=bank[:, 2 * difference + u, :], lhsT=words[:, first : (difference + 1) * K_PASS // 2 : 2],
+                        rhs=identity[:], is_transpose=True, start=True, stop=True,
+                    )
+            nc.scalar.copy(
+                out=grouped[:].rearrange("p d n t -> p (d n t)").bitcast(F32).rearrange(
+                    "p (d n u) -> p d n u", d=STAGE_PASSES, u=2
+                ),
+                in_=bank[:].rearrange("p (d u) n -> p d n u", u=2),
+            )
+
+        def negate(odd, stage):
             minus_odd = step1.tile([P, PACK, P], F32)
-            nc.scalar.activation(out=minus_odd[:], in_=odd, func=COPY, scale=-1.0)
+            if stage % VECTOR_NEGATES_EVERY == VECTOR_NEGATES_EVERY - 1:
+                nc.vector.tensor_scalar_mul(minus_odd[:], odd, -1.0)
+            else:
+                nc.scalar.activation(out=minus_odd[:], in_=odd, func=COPY, scale=-1.0)
             return minus_odd
 
         unread = spare.tile([P, P], F32)
@@ -172,7 +216,7 @@ def tile_waveletlinearlayer_kernel(tc, x, W_words, W_scales, b, out):
             )
             nc.sync.dma_start(out=out[row_tile * P : (row_tile + 1) * P, :], in_=result[:])
 
-        paired_tiles, minus_odds, grouped_tiles, code_tiles = {}, {}, {}, {}
+        paired_tiles, minus_odds, feature_tiles, grouped_tiles, code_tiles = {}, {}, {}, {}, {}
         waiting = []
 
         for warm_up in range(WARM_UP_MATMULS):
@@ -198,17 +242,23 @@ def tile_waveletlinearlayer_kernel(tc, x, W_words, W_scales, b, out):
 
             stage = turn
             if stage < STAGES:
-                paired_tiles[stage] = pair_columns(stage)
+                if on_vector(stage):
+                    feature_tiles[stage] = add_rows(pair_columns_in_rows(stage))
+                else:
+                    paired_tiles[stage] = pair_columns(stage)
 
             stage = turn - NEGATE_LAG
-            if 0 <= stage < STAGES:
-                minus_odds[stage] = negate(paired_tiles[stage][:, ODD])
+            if 0 <= stage < STAGES and not on_vector(stage):
+                minus_odds[stage] = negate(paired_tiles[stage][:, ODD], stage)
 
             stage = turn - TRANSPOSE_LAG
             if 0 <= stage < STAGES:
-                even, odd = paired_tiles[stage][:, EVEN], paired_tiles[stage][:, ODD]
                 grouped = packed.tile([P, STAGE_PASSES, P, PACK], BF16, align_bytes=64)
                 grouped_tiles[stage] = grouped
-                transpose_and_add(even, odd, grouped[:, 0])
-                transpose_and_add(even, minus_odds[stage][:], grouped[:, 1])
-                keep_clock_up(KEEP_ALIVE_COLUMNS)
+                if on_vector(stage):
+                    transpose_words(feature_tiles[stage], grouped)
+                else:
+                    even, odd = paired_tiles[stage][:, EVEN], paired_tiles[stage][:, ODD]
+                    transpose_and_add(even, odd, grouped[:, 0])
+                    transpose_and_add(even, minus_odds[stage][:], grouped[:, 1])
+                    keep_clock_up(KEEP_ALIVE_COLUMNS)

@@ -38,15 +38,15 @@ STAGES = ROW_TILES * TILE_STAGES
 STAGE_PASSES = 2
 RUN_STAGES = 8
 VECTOR_NEGATES_EVERY = 8
-KEEP_ALIVE_COLUMNS = 64
-WARM_UP_MATMULS = 7
+KEEP_ALIVE_COLUMNS = 80
+WARM_UP_MATMULS = 5
 EARLY_PIECES = 5
 HEAD_CHUNKS = 4
 
 NEGATE_LAG = 1
 TRANSPOSE_LAG = 2
-QUANTISE_LAG = 4
-FINISH_LAG = 6
+QUANTISE_LAG = 5
+FINISH_LAG = 7
 
 FLOPS = 2 * BATCH * CHANNELS * PIXELS * OUT
 
@@ -153,9 +153,12 @@ def tile_waveletlinearlayer_kernel(tc, x, W_words, W_scales, b, out):
                 in_=bank[:].rearrange("p (d u) n -> p d n u", u=2),
             )
 
+        def vector_negates(stage):
+            return stage % VECTOR_NEGATES_EVERY == VECTOR_NEGATES_EVERY - 2 and stage < STAGES - VECTOR_NEGATES_EVERY
+
         def negate(odd, stage):
             minus_odd = step1.tile([P, PACK, P], F32)
-            if stage % VECTOR_NEGATES_EVERY == VECTOR_NEGATES_EVERY - 1:
+            if vector_negates(stage):
                 nc.vector.tensor_scalar_mul(minus_odd[:], odd, -1.0)
             else:
                 nc.scalar.activation(out=minus_odd[:], in_=odd, func=COPY, scale=-1.0)
@@ -240,16 +243,16 @@ def tile_waveletlinearlayer_kernel(tc, x, W_words, W_scales, b, out):
             if stage >= 0 and (stage + 1) % TILE_STAGES == 0:
                 finish(stage // TILE_STAGES)
 
+            stage = turn - NEGATE_LAG
+            if 0 <= stage < STAGES and not on_vector(stage):
+                minus_odds[stage] = negate(paired_tiles[stage][:, ODD], stage)
+
             stage = turn
             if stage < STAGES:
                 if on_vector(stage):
                     feature_tiles[stage] = add_rows(pair_columns_in_rows(stage))
                 else:
                     paired_tiles[stage] = pair_columns(stage)
-
-            stage = turn - NEGATE_LAG
-            if 0 <= stage < STAGES and not on_vector(stage):
-                minus_odds[stage] = negate(paired_tiles[stage][:, ODD], stage)
 
             stage = turn - TRANSPOSE_LAG
             if 0 <= stage < STAGES:

from contextlib import ExitStack

import concourse.mybir as mybir
from concourse.masks import make_identity

F32 = mybir.dt.float32
BF16 = mybir.dt.bfloat16
I32 = mybir.dt.int32
U32 = mybir.dt.uint32
U8 = mybir.dt.uint8
FP8X4 = mybir.dt.float8_e4m3fn_x4
FP4X4 = mybir.dt.float4_e2m1fn_x4
ADD = mybir.AluOpType.add
MULT = mybir.AluOpType.mult
SUBTRACT = mybir.AluOpType.subtract
COPY = mybir.ActivationFunctionType.Copy

P = 128
PACK = 4
K_PASS = P * PACK

BATCH, CHANNELS, SIDE, OUT = 256, 4, 64, 128
HALF_SIDE = SIDE // 2
PIXELS = SIDE * SIDE
BAND = HALF_SIDE * HALF_SIDE
SUBBANDS = 4
PASSES = CHANNELS * SUBBANDS * BAND // K_PASS
BAND_PASSES = BAND // K_PASS
PASS_ROWS = HALF_SIDE // BAND_PASSES
PASS_PIXELS = PIXELS // BAND_PASSES
ROW_TILES = BATCH // P
WORDS_PER_ROW = HALF_SIDE // PACK
EVEN, ODD = 0, 1

SIGNS = 2
TILE_STAGES = CHANNELS * BAND_PASSES * SIGNS
STAGES = ROW_TILES * TILE_STAGES
STAGE_PASSES = 2
RUN_STAGES = 8
VECTOR_NEGATES_EVERY = 8
KEEP_ALIVE_COLUMNS = 80
WARM_UP_MATMULS = 5
EARLY_PIECES = 5
HEAD_CHUNKS = 4

NEGATE_LAG = 1
TRANSPOSE_LAG = 2
QUANTISE_LAG = 5
FINISH_LAG = 7

FLOPS = 2 * BATCH * CHANNELS * PIXELS * OUT


def tile_waveletlinearlayer_kernel(tc, x, W_words, W_scales, b, out):
    nc = tc.nc
    with ExitStack() as ctx:
        const = ctx.enter_context(tc.tile_pool(name="const", bufs=1))
        step1 = ctx.enter_context(tc.tile_pool(name="step1", bufs=5))
        step12 = ctx.enter_context(tc.tile_pool(name="step12", bufs=1))
        packed = ctx.enter_context(tc.tile_pool(name="packed", bufs=14))
        results = ctx.enter_context(tc.tile_pool(name="results", bufs=2))
        banks = ctx.enter_context(tc.psum_pool(name="banks", bufs=6))
        sums = ctx.enter_context(tc.psum_pool(name="sums", bufs=1))
        spare = ctx.enter_context(tc.psum_pool(name="spare", bufs=1))
        ctx.enter_context(tc.manual_schedule())

        identity = const.tile([P, P], F32)
        make_identity(nc, identity[:])

        pixel_tiles = {}

        def load_pixels(piece):
            row_tile, columns = divmod(piece, CHANNELS * BAND_PASSES)
            chunks = HEAD_CHUNKS if piece == 0 else 1
            width = PASS_PIXELS // chunks
            pixel_tiles[piece] = []
            for chunk in range(chunks):
                pixels = const.tile([P, width], BF16, name="pixels_%d_%d" % (piece, chunk))
                first = columns * PASS_PIXELS + chunk * width
                nc.sync.dma_start(out=pixels[:], in_=x[row_tile * P : (row_tile + 1) * P, first : first + width])
                pixel_tiles[piece].append(pixels)

        w_scales = const.tile([P, PASSES, OUT], U8, align_bytes=64)
        nc.vector.memset(w_scales[:].bitcast(I32), 0)
        w_codes = const.tile([P, PASSES, 2 * OUT], U8, align_bytes=64)
        bias = const.tile([P, OUT], BF16)

        for piece in range(EARLY_PIECES):
            load_pixels(piece)
        for quadrant in range(4):
            nc.sync.dma_start(
                out=w_scales[32 * quadrant : 32 * quadrant + 4].bitcast(I32),
                in_=W_scales[:, 4 * quadrant : 4 * quadrant + 4, :].bitcast(I32).rearrange("g r w -> r g w"),
            )
        nc.sync.dma_start(out=w_codes[:].bitcast(I32), in_=W_words.bitcast(I32).rearrange("g p w -> p g w"))
        for piece in range(EARLY_PIECES, STAGES // SIGNS):
            load_pixels(piece)
        nc.sync.dma_start(out=bias[:], in_=b.partition_broadcast(P))

        def pair_columns(stage):
            piece, sign = divmod(stage, SIGNS)
            paired = step1.tile([P, 2, PACK, P], F32)
            planes = paired[:].rearrange("n r t (i c) -> n r i c t", c=WORDS_PER_ROW)
            rows = PASS_ROWS // len(pixel_tiles[piece])
            for chunk, chunk_tile in enumerate(pixel_tiles[piece]):
                pixels = chunk_tile[:].rearrange(
                    "n (i r c t e) -> n e r i c t", i=rows, r=2, c=WORDS_PER_ROW, t=PACK, e=2
                )
                nc.vector.tensor_tensor(
                    out=planes[:, :, chunk * rows : (chunk + 1) * rows],
                    in0=pixels[:, 0],
                    in1=pixels[:, 1],
                    op=(ADD if sign == 0 else SUBTRACT),
                )
            return paired

        def on_vector(stage):
            return stage == STAGES - 1

        def pair_columns_in_rows(stage):
            piece, sign = divmod(stage, SIGNS)
            rows = step12.tile([P, PASS_ROWS, 2, HALF_SIDE], F32)
            pixels = pixel_tiles[piece][0][:].rearrange("n (k e) -> n e k", e=2)
            nc.vector.tensor_tensor(
                out=rows[:].rearrange("n i r j -> n (i r j)"), in0=pixels[:, 0], in1=pixels[:, 1],
                op=(ADD if sign == 0 else SUBTRACT),
            )
            return rows

        def add_rows(rows):
            features = step12.tile([P, STAGE_PASSES, K_PASS], BF16, align_bytes=64)
            for difference in range(STAGE_PASSES):
                nc.vector.tensor_tensor(
                    out=features[:, difference].rearrange("n (i j) -> n i j", j=HALF_SIDE),
                    in0=rows[:, :, EVEN], in1=rows[:, :, ODD], op=(SUBTRACT if difference else ADD),
                )
            return features

        def transpose_words(features, grouped):
            words = features[:].rearrange("n d k -> n (d k)").bitcast(F32)
            bank = banks.tile([P, PACK, P], F32)
            for difference in range(STAGE_PASSES):
                for u in range(2):
                    first = difference * K_PASS // 2 + u
                    nc.tensor.matmul(
                        out=bank[:, 2 * difference + u, :], lhsT=words[:, first : (difference + 1) * K_PASS // 2 : 2],
                        rhs=identity[:], is_transpose=True, start=True, stop=True,
                    )
            nc.scalar.copy(
                out=grouped[:].rearrange("p d n t -> p (d n t)").bitcast(F32).rearrange(
                    "p (d n u) -> p d n u", d=STAGE_PASSES, u=2
                ),
                in_=bank[:].rearrange("p (d u) n -> p d n u", u=2),
            )

        def vector_negates(stage):
            return stage % VECTOR_NEGATES_EVERY == VECTOR_NEGATES_EVERY - 2 and stage < STAGES - VECTOR_NEGATES_EVERY

        def negate(odd, stage):
            minus_odd = step1.tile([P, PACK, P], F32)
            if vector_negates(stage):
                nc.vector.tensor_scalar_mul(minus_odd[:], odd, -1.0)
            else:
                nc.scalar.activation(out=minus_odd[:], in_=odd, func=COPY, scale=-1.0)
            return minus_odd

        unread = spare.tile([P, P], F32)

        def keep_clock_up(columns):
            nc.tensor.matmul(
                out=unread[:, :columns], lhsT=identity[:], rhs=identity[:, :columns], start=True, stop=True
            )

        def transpose_and_add(first, second, target):
            bank = banks.tile([P, PACK, P], F32)
            for t in range(PACK):
                for addend in (first, second):
                    nc.tensor.matmul(
                        out=bank[:, t, :], lhsT=addend[:, t, :], rhs=identity[:], is_transpose=True,
                        start=(addend is first), stop=(addend is second),
                    )
            nc.scalar.copy(out=target, in_=bank[:].rearrange("p t n -> p n t"))

        def quantise(grouped):
            t_codes = packed.tile([P, STAGE_PASSES, P], U32, align_bytes=64)
            t_scales = packed.tile([P, STAGE_PASSES, P], U8, align_bytes=64)
            nc.vector.quantize_mx(
                out=t_codes[:].rearrange("p s n -> p (s n)").bitcast(FP8X4),
                scales=t_scales[:].rearrange("p s n -> p (s n)"),
                in_=grouped[:].rearrange("p s n t -> p (s n t)"),
            )
            return t_codes, t_scales

        sum_tiles = {}

        def multiply(stage, t_codes, t_scales):
            row_tile, tile_stage = divmod(stage, TILE_STAGES)
            channel, rest = divmod(tile_stage, BAND_PASSES * SIGNS)
            half, sign = divmod(rest, SIGNS)
            if tile_stage == 0:
                sum_tiles[row_tile] = sums.tile([P, OUT], F32, name="batch_sum")
            for difference in range(STAGE_PASSES):
                subband = 2 * sign + difference
                g = (channel * SUBBANDS + subband) * BAND_PASSES + half
                nc.tensor.matmul_mx(
                    out=sum_tiles[row_tile][:],
                    lhsT=t_codes[:, difference, :].bitcast(FP8X4),
                    lhsT_scale=t_scales[:, difference, :],
                    rhs=w_codes[:, g, :].bitcast(FP4X4),
                    rhs_scale=w_scales[:, g, :],
                    start=(tile_stage == 0 and difference == 0),
                    stop=(tile_stage == TILE_STAGES - 1 and difference == STAGE_PASSES - 1),
                )

        def finish(row_tile):
            result = results.tile([P, OUT], F32)
            nc.vector.scalar_tensor_tensor(
                out=result[:], in0=sum_tiles[row_tile][:], scalar=0.5, in1=bias[:], op0=MULT, op1=ADD
            )
            nc.sync.dma_start(out=out[row_tile * P : (row_tile + 1) * P, :], in_=result[:])

        paired_tiles, minus_odds, feature_tiles, grouped_tiles, code_tiles = {}, {}, {}, {}, {}
        waiting = []

        for warm_up in range(WARM_UP_MATMULS):
            keep_clock_up(P)
        for turn in range(STAGES + FINISH_LAG + 1):
            stage = turn - QUANTISE_LAG
            if 0 <= stage < STAGES:
                code_tiles[stage] = quantise(grouped_tiles[stage])
                waiting.append(stage)
            if turn >= STAGES + TRANSPOSE_LAG:
                run = len(waiting)
            elif len(waiting) > RUN_STAGES:
                run = RUN_STAGES
            else:
                run = 0
            for ready in waiting[:run]:
                multiply(ready, code_tiles[ready][0], code_tiles[ready][1])
            waiting = waiting[run:]

            stage = turn - FINISH_LAG
            if stage >= 0 and (stage + 1) % TILE_STAGES == 0:
                finish(stage // TILE_STAGES)

            stage = turn - NEGATE_LAG
            if 0 <= stage < STAGES and not on_vector(stage):
                minus_odds[stage] = negate(paired_tiles[stage][:, ODD], stage)

            stage = turn
            if stage < STAGES:
                if on_vector(stage):
                    feature_tiles[stage] = add_rows(pair_columns_in_rows(stage))
                else:
                    paired_tiles[stage] = pair_columns(stage)

            stage = turn - TRANSPOSE_LAG
            if 0 <= stage < STAGES:
                grouped = packed.tile([P, STAGE_PASSES, P, PACK], BF16, align_bytes=64)
                grouped_tiles[stage] = grouped
                if on_vector(stage):
                    transpose_words(feature_tiles[stage], grouped)
                else:
                    even, odd = paired_tiles[stage][:, EVEN], paired_tiles[stage][:, ODD]
                    transpose_and_add(even, odd, grouped[:, 0])
                    transpose_and_add(even, minus_odds[stage][:], grouped[:, 1])
                    keep_clock_up(KEEP_ALIVE_COLUMNS)
